import numpy as np
import ml_dtypes


def mxq(x, axis, fmt="e4m3"):
    dtype, down = {"e4m3": (ml_dtypes.float8_e4m3fn, 7), "e5m2": (ml_dtypes.float8_e5m2, 14)}[fmt]
    v = np.moveaxis(np.asarray(x, np.float32).astype(ml_dtypes.bfloat16).astype(np.float64), axis, -1)
    blocks = v.reshape(v.shape[:-1] + (-1, 32))
    amax = np.abs(blocks).max(-1, keepdims=True)
    byte = np.maximum(np.where(amax > 0, np.frexp(amax)[1] - 1 + 127, 0) - down, 1)
    scale = np.exp2(byte - 127.0)
    codes = (blocks / scale).astype(np.float32).astype(dtype).astype(np.float64)
    return np.moveaxis((codes * scale).reshape(v.shape), -1, axis)


WIDE = False


def mx_kscale(k):
    if not WIDE:
        return np.ones(k)
    levels = np.array([10, -10, 5, -5, 0])
    if k % 512:
        return np.exp2(np.random.permutation(np.resize(levels, k // 32))).repeat(32)
    a = np.empty((k // 512, 16))
    for p in range(k // 512):
        a[p, :8] = np.random.permutation(np.resize(levels, 8))
        for g in range(8):
            far = levels[np.abs(levels - a[p, g]) >= 10]
            a[p, g + 8] = far[np.random.randint(len(far))]
    return np.exp2(a.ravel()).repeat(32)


BF16 = ml_dtypes.bfloat16


def bf(x):
    return np.asarray(x, np.float32).astype(BF16)


def f64(x):
    return np.asarray(x).astype(np.float64)


B, IN_F, OUT_F = 128, 65536, 512
IN_Q = IN_F // 4
OUT_Q = OUT_F // 4


def setup_inputs():
    s = mx_kscale(IN_Q)
    scale = 1.0 / np.sqrt(IN_Q)
    inp = {"x": bf((np.random.standard_normal((B, 4, IN_Q)) * s).reshape(B, IN_F))}
    for name in ["rr", "ri", "rj", "rk"]:
        inp["W_" + name] = bf(np.random.uniform(-scale, scale, (OUT_Q, IN_Q)) / s[None, :])
    for name in ["rr", "ri", "rj", "rk"]:
        inp["b_" + name] = bf(np.random.standard_normal(OUT_Q) * 0.5)
    return inp


def reference(x, W_rr, W_ri, W_rj, W_rk, b_rr, b_ri, b_rj, b_rk):
    b = x.shape[0]
    xs = f64(x).reshape(b, 4, IN_Q)
    W = np.stack([f64(W_rr), f64(W_ri), f64(W_rj), f64(W_rk)])
    bias = np.stack([f64(b_rr), f64(b_ri), f64(b_rj), f64(b_rk)])
    xq = mxq(xs, 2, "e4m3")
    Wq = mxq(W, 2, "e4m3")
    Y = (xq.reshape(b * 4, IN_Q) @ Wq.reshape(4 * OUT_Q, IN_Q).T).reshape(b, 4, 4, OUT_Q) + bias
    out_r = Y[:, 0, 0] - Y[:, 1, 1] - Y[:, 2, 2] - Y[:, 3, 3]
    out_i = Y[:, 0, 1] + Y[:, 1, 0] + Y[:, 2, 3] - Y[:, 3, 2]
    out_j = Y[:, 0, 2] - Y[:, 1, 3] + Y[:, 2, 0] + Y[:, 3, 1]
    out_k = Y[:, 0, 3] + Y[:, 1, 2] - Y[:, 2, 1] + Y[:, 3, 0]
    out = np.stack([out_r, out_i, out_j, out_k], axis=1)
    return out.reshape(b, -1)

@@ -1,0 +1,168 @@
+from contextlib import ExitStack
+
+import concourse.masks as masks
+import concourse.mybir as mybir
+
+F32 = mybir.dt.float32
+BF16 = mybir.dt.bfloat16
+U32 = mybir.dt.uint32
+U8 = mybir.dt.uint8
+FP8X4 = mybir.dt.float8_e4m3fn_x4
+ADD = mybir.AluOpType.add
+SUBTRACT = mybir.AluOpType.subtract
+
+P = 128
+MEMBERS = 4
+K = 16384
+PACK = 4
+K_PASS = P * PACK
+PASSES = K // K_PASS
+HALVES = 2
+BANK_WORDS = 512
+BANK_MEMBERS = BANK_WORDS // (HALVES * P)
+
+STAGE_PASSES = 1
+STAGES = PASSES // STAGE_PASSES
+LOAD_PASSES = 2
+LOAD_COLS = LOAD_PASSES * K_PASS
+RAW_BUFS = 6
+VECTOR_EVERY = 4
+
+SIGN = (
+    (1, -1, -1, -1),
+    (1, 1, 1, -1),
+    (1, -1, 1, 1),
+    (1, 1, -1, 1),
+)
+
+FLOPS = 2 * (MEMBERS * P) * (MEMBERS * P) * K
+
+
+def tile_qdense_k_kernel(
+    tc, x, W_rr, W_ri, W_rj, W_rk, b_rr, b_ri, b_rj, b_rk, out
+):
+    nc = tc.nc
+    x_chunks = x.rearrange("b (c k) -> b c k", c=MEMBERS)
+    weights = (W_rr, W_ri, W_rj, W_rk)
+    biases = (b_rr, b_ri, b_rj, b_rk)
+
+    with ExitStack() as ctx:
+        ctx.enter_context(tc.manual_schedule())
+        const = ctx.enter_context(tc.tile_pool(name="const", bufs=1))
+        raw_pool = ctx.enter_context(tc.tile_pool(name="raw", bufs=RAW_BUFS))
+        grouped_pool = ctx.enter_context(tc.tile_pool(name="grouped", bufs=4))
+        code_pool = ctx.enter_context(tc.tile_pool(name="codes", bufs=3))
+        product_pool = ctx.enter_context(tc.psum_pool(name="products", bufs=1))
+        bank_pool = ctx.enter_context(tc.psum_pool(name="banks", bufs=4))
+
+        def add_chunk(total, terms, c):
+            for j in range(MEMBERS):
+                nc.vector.tensor_tensor(
+                    out=total[:, j, :],
+                    in0=total[:, j, :],
+                    in1=terms[:, j ^ c, :],
+                    op=ADD if SIGN[j][c] > 0 else SUBTRACT,
+                )
+
+        identity = const.tile([P, P], F32)
+        masks.make_identity(nc, identity[:])
+
+        ones = const.tile([P, P], BF16)
+        nc.vector.memset(ones[:], 1.0)
+        bias_rows = const.tile([P, MEMBERS, P], BF16)
+        nc.vector.memset(bias_rows[:], 0.0)
+        for q in range(MEMBERS):
+            nc.scalar.dma_start(out=bias_rows[0:1, q, :], in_=biases[q].unsqueeze(0))
+        bias_bank = bank_pool.tile([P, MEMBERS, P], F32, tag="bank")
+        nc.tensor.matmul(
+            out=bias_bank[:].rearrange("p q o -> p (q o)"),
+            lhsT=ones[:],
+            rhs=bias_rows[:].rearrange("p q o -> p (q o)"),
+            start=True,
+            stop=True,
+        )
+        total = const.tile([P, MEMBERS, P], F32)
+        nc.vector.tensor_copy(out=total[:], in_=bias_bank[:])
+        for c in range(1, MEMBERS):
+            add_chunk(total, bias_bank, c)
+
+        products = [
+            product_pool.tile([P, MEMBERS, P], F32, name="products%d" % c)
+            for c in range(MEMBERS)
+        ]
+
+        def transpose_pass(raw, pass_in_load, unit):
+            grouped = grouped_pool.tile([P, MEMBERS * P * PACK], BF16, align_bytes=64)
+            grouped_words = grouped[:].bitcast(F32)
+            for b in range(MEMBERS // BANK_MEMBERS):
+                bank = bank_pool.tile([P, BANK_MEMBERS, HALVES, P], F32, tag="bank")
+                for i in range(BANK_MEMBERS):
+                    for u in range(HALVES):
+                        first = pass_in_load * K_PASS
+                        words = raw[:, b * BANK_MEMBERS + i, first : first + K_PASS].bitcast(F32)
+                        nc.tensor.transpose(bank[:, i, u, :], words[:, u::HALVES], identity[:])
+                bank_number = unit * (MEMBERS // BANK_MEMBERS) + b
+                to_vector = bank_number % VECTOR_EVERY == VECTOR_EVERY - 1
+                copy_out = nc.vector.tensor_copy if to_vector else nc.scalar.copy
+                copy_out(
+                    out=grouped_words[:, b * BANK_WORDS : (b + 1) * BANK_WORDS].rearrange(
+                        "p (i r u) -> p i r u", i=BANK_MEMBERS, u=HALVES
+                    ),
+                    in_=bank[:].rearrange("p i u r -> p i r u"),
+                )
+            return grouped
+
+        def quantise(grouped, codes, scales):
+            nc.vector.quantize_mx(out=codes.bitcast(FP8X4), scales=scales, in_=grouped[:])
+
+        def multiply(stage, x_codes, x_scales, w_codes, w_scales):
+            for c in range(MEMBERS):
+                rows = slice(c * P, (c + 1) * P)
+                for g in range(STAGE_PASSES):
+                    number = stage * STAGE_PASSES + g
+                    nc.tensor.matmul_mx(
+                        out=products[c][:].rearrange("p q o -> p (q o)"),
+                        lhsT=x_codes[:, g, rows].bitcast(FP8X4),
+                        lhsT_scale=x_scales[:, g, rows],
+                        rhs=w_codes[:, g, :].bitcast(FP8X4),
+                        rhs_scale=w_scales[:, g, :],
+                        start=(number == 0),
+                        stop=(number == PASSES - 1),
+                    )
+
+        waiting = None
+        ready = None
+        unit = 0
+        x_raw = None
+        w_raw = None
+        for stage in range(STAGES):
+            first_pass = stage * STAGE_PASSES
+            if first_pass % LOAD_PASSES == 0:
+                cols = slice(first_pass * K_PASS, first_pass * K_PASS + LOAD_COLS)
+                x_raw = raw_pool.tile([P, MEMBERS, LOAD_COLS], BF16, name="x_raw")
+                nc.sync.dma_start(out=x_raw[:], in_=x_chunks[:, :, cols])
+                w_raw = raw_pool.tile([P, MEMBERS, LOAD_COLS], BF16, name="w_raw")
+                for q in range(MEMBERS):
+                    nc.sync.dma_start(out=w_raw[:, q, :], in_=weights[q][:, cols])
+
+            x_codes = code_pool.tile([P, STAGE_PASSES, MEMBERS * P], U32, align_bytes=64)
+            x_scales = code_pool.tile([P, STAGE_PASSES, MEMBERS * P], U8, align_bytes=64)
+            w_codes = code_pool.tile([P, STAGE_PASSES, MEMBERS * P], U32, align_bytes=64)
+            w_scales = code_pool.tile([P, STAGE_PASSES, MEMBERS * P], U8, align_bytes=64)
+
+            for raw, codes, scales in ((x_raw, x_codes, x_scales), (w_raw, w_codes, w_scales)):
+                for g in range(STAGE_PASSES):
+                    grouped = transpose_pass(raw, (first_pass + g) % LOAD_PASSES, unit)
+                    unit += 1
+                    if waiting is not None:
+                        quantise(*waiting)
+                    waiting = (grouped, codes[:, g, :], scales[:, g, :])
+            if ready is not None:
+                multiply(stage - 1, *ready)
+            ready = (x_codes, x_scales, w_codes, w_scales)
+        quantise(*waiting)
+        multiply(STAGES - 1, *ready)
+
+        for c in range(MEMBERS):
+            add_chunk(total, products[c], c)
+        nc.sync.dma_start(out=out, in_=total[:].rearrange("p j o -> p (j o)"))

@@ -18,6 +18,8 @@ PACK = 4
 K_PASS = P * PACK
 PASSES = K // K_PASS
 HALVES = 2
+K_HALF = K_PASS // HALVES
+RUN = 16
 BANK_WORDS = 512
 BANK_MEMBERS = BANK_WORDS // (HALVES * P)
 
@@ -26,7 +28,7 @@ STAGES = PASSES // STAGE_PASSES
 LOAD_PASSES = 2
 LOAD_COLS = LOAD_PASSES * K_PASS
 RAW_BUFS = 6
-VECTOR_EVERY = 4
+SORTS = 2
 
 SIGN = (
     (1, -1, -1, -1),
@@ -50,6 +52,7 @@ def tile_qdense_k_kernel(
         ctx.enter_context(tc.manual_schedule())
         const = ctx.enter_context(tc.tile_pool(name="const", bufs=1))
         raw_pool = ctx.enter_context(tc.tile_pool(name="raw", bufs=RAW_BUFS))
+        sorted_pool = ctx.enter_context(tc.tile_pool(name="sorted", bufs=2))
         grouped_pool = ctx.enter_context(tc.tile_pool(name="grouped", bufs=4))
         code_pool = ctx.enter_context(tc.tile_pool(name="codes", bufs=3))
         product_pool = ctx.enter_context(tc.psum_pool(name="products", bufs=1))
@@ -91,20 +94,30 @@ def tile_qdense_k_kernel(
             for c in range(MEMBERS)
         ]
 
-        def transpose_pass(raw, pass_in_load, unit):
+        def sort_words(raw, halves, part):
+            width = MEMBERS * LOAD_COLS // SORTS
+            source = raw[:, part * width : (part + 1) * width]
+            target = halves[:, :, part * width // HALVES : (part + 1) * width // HALVES]
+            nc.vector.tensor_copy(
+                out=target.rearrange("p u (g e) -> p u g e", e=RUN),
+                in_=source.rearrange("p (g u e) -> p u g e", u=HALVES, e=RUN),
+            )
+
+        def transpose_pass(halves, pass_in_load):
             grouped = grouped_pool.tile([P, MEMBERS * P * PACK], BF16, align_bytes=64)
             grouped_words = grouped[:].bitcast(F32)
             for b in range(MEMBERS // BANK_MEMBERS):
                 bank = bank_pool.tile([P, BANK_MEMBERS, HALVES, P], F32, tag="bank")
                 for i in range(BANK_MEMBERS):
+                    member = b * BANK_MEMBERS + i
+                    first = (member * LOAD_PASSES + pass_in_load) * K_HALF
                     for u in range(HALVES):
-                        first = pass_in_load * K_PASS
-                        words = raw[:, b * BANK_MEMBERS + i, first : first + K_PASS].bitcast(F32)
-                        nc.tensor.transpose(bank[:, i, u, :], words[:, u::HALVES], identity[:])
-                bank_number = unit * (MEMBERS // BANK_MEMBERS) + b
-                to_vector = bank_number % VECTOR_EVERY == VECTOR_EVERY - 1
-                copy_out = nc.vector.tensor_copy if to_vector else nc.scalar.copy
-                copy_out(
+                        nc.tensor.transpose(
+                            bank[:, i, u, :],
+                            halves[:, u, first : first + K_HALF].bitcast(F32),
+                            identity[:],
+                        )
+                nc.scalar.copy(
                     out=grouped_words[:, b * BANK_WORDS : (b + 1) * BANK_WORDS].rearrange(
                         "p (i r u) -> p i r u", i=BANK_MEMBERS, u=HALVES
                     ),
@@ -130,33 +143,54 @@ def tile_qdense_k_kernel(
                         stop=(number == PASSES - 1),
                     )
 
+        def load(number):
+            cols = slice(number * LOAD_COLS, (number + 1) * LOAD_COLS)
+            x_raw = raw_pool.tile([P, MEMBERS * LOAD_COLS], BF16, name="x_raw")
+            nc.sync.dma_start(
+                out=x_raw[:].rearrange("p (m k) -> p m k", m=MEMBERS), in_=x_chunks[:, :, cols]
+            )
+            w_raw = raw_pool.tile([P, MEMBERS * LOAD_COLS], BF16, name="w_raw")
+            for q in range(MEMBERS):
+                nc.sync.dma_start(
+                    out=w_raw[:, q * LOAD_COLS : (q + 1) * LOAD_COLS], in_=weights[q][:, cols]
+                )
+            half_shape = [P, HALVES, MEMBERS * LOAD_COLS // HALVES]
+            x_halves = sorted_pool.tile(half_shape, BF16, name="x_halves")
+            w_halves = sorted_pool.tile(half_shape, BF16, name="w_halves")
+            return (x_raw, x_halves), (w_raw, w_halves)
+
         waiting = None
         ready = None
-        unit = 0
-        x_raw = None
-        w_raw = None
+        current = None
+        coming = load(0)
+        sorts = [(pair, part) for pair in coming for part in range(SORTS)]
         for stage in range(STAGES):
-            first_pass = stage * STAGE_PASSES
-            if first_pass % LOAD_PASSES == 0:
-                cols = slice(first_pass * K_PASS, first_pass * K_PASS + LOAD_COLS)
-                x_raw = raw_pool.tile([P, MEMBERS, LOAD_COLS], BF16, name="x_raw")
-                nc.sync.dma_start(out=x_raw[:], in_=x_chunks[:, :, cols])
-                w_raw = raw_pool.tile([P, MEMBERS, LOAD_COLS], BF16, name="w_raw")
-                for q in range(MEMBERS):
-                    nc.sync.dma_start(out=w_raw[:, q, :], in_=weights[q][:, cols])
+            if stage % LOAD_PASSES == 0:
+                for (raw, halves), part in sorts:
+                    sort_words(raw, halves, part)
+                current = coming
+                sorts = []
+                if stage + LOAD_PASSES < STAGES:
+                    coming = load(stage // LOAD_PASSES + 1)
+                    sorts = [(pair, part) for pair in coming for part in range(SORTS)]
 
             x_codes = code_pool.tile([P, STAGE_PASSES, MEMBERS * P], U32, align_bytes=64)
             x_scales = code_pool.tile([P, STAGE_PASSES, MEMBERS * P], U8, align_bytes=64)
             w_codes = code_pool.tile([P, STAGE_PASSES, MEMBERS * P], U32, align_bytes=64)
             w_scales = code_pool.tile([P, STAGE_PASSES, MEMBERS * P], U8, align_bytes=64)
 
-            for raw, codes, scales in ((x_raw, x_codes, x_scales), (w_raw, w_codes, w_scales)):
-                for g in range(STAGE_PASSES):
-                    grouped = transpose_pass(raw, (first_pass + g) % LOAD_PASSES, unit)
-                    unit += 1
-                    if waiting is not None:
-                        quantise(*waiting)
-                    waiting = (grouped, codes[:, g, :], scales[:, g, :])
+            for (raw, halves), codes, scales in (
+                (current[0], x_codes, x_scales),
+                (current[1], w_codes, w_scales),
+            ):
+                grouped = transpose_pass(halves, stage % LOAD_PASSES)
+                if waiting is not None:
+                    quantise(*waiting)
+                waiting = (grouped, codes[:, 0, :], scales[:, 0, :])
+                if sorts:
+                    (next_raw, next_halves), part = sorts[0]
+                    sorts = sorts[1:]
+                    sort_words(next_raw, next_halves, part)
             if ready is not None:
                 multiply(stage - 1, *ready)
             ready = (x_codes, x_scales, w_codes, w_scales)

@@ -99,8 +99,8 @@ def tile_qdense_k_kernel(
             source = raw[:, part * width : (part + 1) * width]
             target = halves[:, :, part * width // HALVES : (part + 1) * width // HALVES]
             nc.vector.tensor_copy(
-                out=target.rearrange("p u (g e) -> p u g e", e=RUN),
-                in_=source.rearrange("p (g u e) -> p u g e", u=HALVES, e=RUN),
+                out=target.rearrange("p u (g e) -> p g u e", e=RUN),
+                in_=source.rearrange("p (g u e) -> p g u e", u=HALVES, e=RUN),
             )
 
         def transpose_pass(halves, pass_in_load):

@@ -12,6 +12,7 @@ ADD = mybir.AluOpType.add
 SUBTRACT = mybir.AluOpType.subtract
 
 P = 128
+QUADRANT = 32
 MEMBERS = 4
 K = 16384
 PACK = 4
@@ -23,12 +24,10 @@ RUN = 16
 BANK_WORDS = 512
 BANK_MEMBERS = BANK_WORDS // (HALVES * P)
 
-STAGE_PASSES = 1
-STAGES = PASSES // STAGE_PASSES
-LOAD_PASSES = 2
-LOAD_COLS = LOAD_PASSES * K_PASS
+LOAD_PASSES = (1, 1) + ((PASSES - 2) // 2) * (2,)
 RAW_BUFS = 6
-SORTS = 2
+VECTOR_EVERY = 8
+BIAS_PASS = 4
 
 SIGN = (
     (1, -1, -1, -1),
@@ -52,72 +51,87 @@ def tile_qdense_k_kernel(
         ctx.enter_context(tc.manual_schedule())
         const = ctx.enter_context(tc.tile_pool(name="const", bufs=1))
         raw_pool = ctx.enter_context(tc.tile_pool(name="raw", bufs=RAW_BUFS))
-        sorted_pool = ctx.enter_context(tc.tile_pool(name="sorted", bufs=2))
+        sorted_pool = ctx.enter_context(tc.tile_pool(name="sorted", bufs=4))
         grouped_pool = ctx.enter_context(tc.tile_pool(name="grouped", bufs=4))
         code_pool = ctx.enter_context(tc.tile_pool(name="codes", bufs=3))
         product_pool = ctx.enter_context(tc.psum_pool(name="products", bufs=1))
         bank_pool = ctx.enter_context(tc.psum_pool(name="banks", bufs=4))
 
-        def add_chunk(total, terms, c):
-            for j in range(MEMBERS):
-                nc.vector.tensor_tensor(
-                    out=total[:, j, :],
-                    in0=total[:, j, :],
-                    in1=terms[:, j ^ c, :],
-                    op=ADD if SIGN[j][c] > 0 else SUBTRACT,
-                )
+        def load(first_pass, passes):
+            width = passes * K_PASS
+            cols = slice(first_pass * K_PASS, first_pass * K_PASS + width)
+            x_raw = raw_pool.tile([P, MEMBERS, max(LOAD_PASSES) * K_PASS], BF16, name="x_raw")
+            nc.sync.dma_start(out=x_raw[:, :, :width], in_=x_chunks[:, :, cols])
+            w_raw = raw_pool.tile([P, MEMBERS, max(LOAD_PASSES) * K_PASS], BF16, name="w_raw")
+            for q in range(MEMBERS):
+                nc.sync.dma_start(out=w_raw[:, q, :width], in_=weights[q][:, cols])
+            return [
+                (x_raw[:, :, g * K_PASS : (g + 1) * K_PASS], w_raw[:, :, g * K_PASS : (g + 1) * K_PASS])
+                for g in range(passes)
+            ]
+
+        raw_passes = []
+        for passes in LOAD_PASSES[:2]:
+            raw_passes.extend(load(len(raw_passes), passes))
 
         identity = const.tile([P, P], F32)
         masks.make_identity(nc, identity[:])
 
-        ones = const.tile([P, P], BF16)
-        nc.vector.memset(ones[:], 1.0)
-        bias_rows = const.tile([P, MEMBERS, P], BF16)
-        nc.vector.memset(bias_rows[:], 0.0)
+        bias_rows = const.tile([P, P], BF16)
+        nc.gpsimd.memset(bias_rows[:], 0.0)
         for q in range(MEMBERS):
-            nc.scalar.dma_start(out=bias_rows[0:1, q, :], in_=biases[q].unsqueeze(0))
-        bias_bank = bank_pool.tile([P, MEMBERS, P], F32, tag="bank")
-        nc.tensor.matmul(
-            out=bias_bank[:].rearrange("p q o -> p (q o)"),
-            lhsT=ones[:],
-            rhs=bias_rows[:].rearrange("p q o -> p (q o)"),
-            start=True,
-            stop=True,
-        )
+            nc.sync.dma_start(
+                out=bias_rows[QUADRANT * q : QUADRANT * q + 1, :], in_=biases[q].unsqueeze(0)
+            )
+        bias_signs = const.tile([P, MEMBERS], BF16)
+        for q in range(MEMBERS):
+            for j in range(MEMBERS):
+                nc.gpsimd.memset(
+                    bias_signs[QUADRANT * q : QUADRANT * (q + 1), j : j + 1],
+                    float(SIGN[j][j ^ q]),
+                )
         total = const.tile([P, MEMBERS, P], F32)
-        nc.vector.tensor_copy(out=total[:], in_=bias_bank[:])
-        for c in range(1, MEMBERS):
-            add_chunk(total, bias_bank, c)
+
+        def sum_biases():
+            bank = bank_pool.tile([P, MEMBERS, P], F32, tag="bank")
+            for j in range(MEMBERS):
+                nc.tensor.matmul(
+                    out=bank[:, j, :],
+                    lhsT=bias_signs[:, j : j + 1].to_broadcast([P, P]),
+                    rhs=bias_rows[:],
+                    start=True,
+                    stop=True,
+                )
+            nc.scalar.copy(out=total[:], in_=bank[:])
 
         products = [
             product_pool.tile([P, MEMBERS, P], F32, name="products%d" % c)
             for c in range(MEMBERS)
         ]
 
-        def sort_words(raw, halves, part):
-            width = MEMBERS * LOAD_COLS // SORTS
-            source = raw[:, part * width : (part + 1) * width]
-            target = halves[:, :, part * width // HALVES : (part + 1) * width // HALVES]
+        def sort_words(raw):
+            halves = sorted_pool.tile([P, HALVES, MEMBERS, K_HALF], BF16, name="halves")
             nc.vector.tensor_copy(
-                out=target.rearrange("p u (g e) -> p g u e", e=RUN),
-                in_=source.rearrange("p (g u e) -> p g u e", u=HALVES, e=RUN),
+                out=halves[:].rearrange("p u m (n e) -> p m n u e", e=RUN),
+                in_=raw.rearrange("p m (n u e) -> p m n u e", u=HALVES, e=RUN),
             )
+            return halves
 
-        def transpose_pass(halves, pass_in_load):
+        def transpose_pass(halves, first_bank):
             grouped = grouped_pool.tile([P, MEMBERS * P * PACK], BF16, align_bytes=64)
             grouped_words = grouped[:].bitcast(F32)
             for b in range(MEMBERS // BANK_MEMBERS):
                 bank = bank_pool.tile([P, BANK_MEMBERS, HALVES, P], F32, tag="bank")
                 for i in range(BANK_MEMBERS):
-                    member = b * BANK_MEMBERS + i
-                    first = (member * LOAD_PASSES + pass_in_load) * K_HALF
                     for u in range(HALVES):
                         nc.tensor.transpose(
                             bank[:, i, u, :],
-                            halves[:, u, first : first + K_HALF].bitcast(F32),
+                            halves[:, u, b * BANK_MEMBERS + i, :].bitcast(F32),
                             identity[:],
                         )
-                nc.scalar.copy(
+                to_vector = (first_bank + b) % VECTOR_EVERY == VECTOR_EVERY - 2
+                copy_out = nc.vector.tensor_copy if to_vector else nc.scalar.copy
+                copy_out(
                     out=grouped_words[:, b * BANK_WORDS : (b + 1) * BANK_WORDS].rearrange(
                         "p (i r u) -> p i r u", i=BANK_MEMBERS, u=HALVES
                     ),
@@ -126,77 +140,57 @@ def tile_qdense_k_kernel(
             return grouped
 
         def quantise(grouped, codes, scales):
-            nc.vector.quantize_mx(out=codes.bitcast(FP8X4), scales=scales, in_=grouped[:])
+            nc.vector.quantize_mx(out=codes[:].bitcast(FP8X4), scales=scales[:], in_=grouped[:])
 
-        def multiply(stage, x_codes, x_scales, w_codes, w_scales):
+        def multiply(number, x_codes, x_scales, w_codes, w_scales):
             for c in range(MEMBERS):
                 rows = slice(c * P, (c + 1) * P)
-                for g in range(STAGE_PASSES):
-                    number = stage * STAGE_PASSES + g
-                    nc.tensor.matmul_mx(
-                        out=products[c][:].rearrange("p q o -> p (q o)"),
-                        lhsT=x_codes[:, g, rows].bitcast(FP8X4),
-                        lhsT_scale=x_scales[:, g, rows],
-                        rhs=w_codes[:, g, :].bitcast(FP8X4),
-                        rhs_scale=w_scales[:, g, :],
-                        start=(number == 0),
-                        stop=(number == PASSES - 1),
-                    )
-
-        def load(number):
-            cols = slice(number * LOAD_COLS, (number + 1) * LOAD_COLS)
-            x_raw = raw_pool.tile([P, MEMBERS * LOAD_COLS], BF16, name="x_raw")
-            nc.sync.dma_start(
-                out=x_raw[:].rearrange("p (m k) -> p m k", m=MEMBERS), in_=x_chunks[:, :, cols]
-            )
-            w_raw = raw_pool.tile([P, MEMBERS * LOAD_COLS], BF16, name="w_raw")
-            for q in range(MEMBERS):
-                nc.sync.dma_start(
-                    out=w_raw[:, q * LOAD_COLS : (q + 1) * LOAD_COLS], in_=weights[q][:, cols]
+                nc.tensor.matmul_mx(
+                    out=products[c][:].rearrange("p q o -> p (q o)"),
+                    lhsT=x_codes[:, rows].bitcast(FP8X4),
+                    lhsT_scale=x_scales[:, rows],
+                    rhs=w_codes[:].bitcast(FP8X4),
+                    rhs_scale=w_scales[:],
+                    start=(number == 0),
+                    stop=(number == PASSES - 1),
                 )
-            half_shape = [P, HALVES, MEMBERS * LOAD_COLS // HALVES]
-            x_halves = sorted_pool.tile(half_shape, BF16, name="x_halves")
-            w_halves = sorted_pool.tile(half_shape, BF16, name="w_halves")
-            return (x_raw, x_halves), (w_raw, w_halves)
 
         waiting = None
         ready = None
-        current = None
-        coming = load(0)
-        sorts = [(pair, part) for pair in coming for part in range(SORTS)]
-        for stage in range(STAGES):
-            if stage % LOAD_PASSES == 0:
-                for (raw, halves), part in sorts:
-                    sort_words(raw, halves, part)
-                current = coming
-                sorts = []
-                if stage + LOAD_PASSES < STAGES:
-                    coming = load(stage // LOAD_PASSES + 1)
-                    sorts = [(pair, part) for pair in coming for part in range(SORTS)]
-
-            x_codes = code_pool.tile([P, STAGE_PASSES, MEMBERS * P], U32, align_bytes=64)
-            x_scales = code_pool.tile([P, STAGE_PASSES, MEMBERS * P], U8, align_bytes=64)
-            w_codes = code_pool.tile([P, STAGE_PASSES, MEMBERS * P], U32, align_bytes=64)
-            w_scales = code_pool.tile([P, STAGE_PASSES, MEMBERS * P], U8, align_bytes=64)
-
-            for (raw, halves), codes, scales in (
-                (current[0], x_codes, x_scales),
-                (current[1], w_codes, w_scales),
-            ):
-                grouped = transpose_pass(halves, stage % LOAD_PASSES)
+        loads = 2
+        halves = [sort_words(raw) for raw in raw_passes[0]]
+        for number in range(PASSES):
+            if loads < len(LOAD_PASSES) and len(raw_passes) < number + 2 + LOAD_PASSES[loads]:
+                raw_passes.extend(load(len(raw_passes), LOAD_PASSES[loads]))
+                loads += 1
+            x_codes = code_pool.tile([P, MEMBERS * P], U32, align_bytes=64)
+            x_scales = code_pool.tile([P, MEMBERS * P], U8, align_bytes=64)
+            w_codes = code_pool.tile([P, MEMBERS * P], U32, align_bytes=64)
+            w_scales = code_pool.tile([P, MEMBERS * P], U8, align_bytes=64)
+            next_halves = []
+            for operand, (codes, scales) in enumerate(((x_codes, x_scales), (w_codes, w_scales))):
+                first_bank = (2 * number + operand) * (MEMBERS // BANK_MEMBERS)
+                grouped = transpose_pass(halves[operand], first_bank)
                 if waiting is not None:
                     quantise(*waiting)
-                waiting = (grouped, codes[:, 0, :], scales[:, 0, :])
-                if sorts:
-                    (next_raw, next_halves), part = sorts[0]
-                    sorts = sorts[1:]
-                    sort_words(next_raw, next_halves, part)
+                waiting = (grouped, codes, scales)
+                if number + 1 < PASSES:
+                    next_halves.append(sort_words(raw_passes[number + 1][operand]))
+            if number == BIAS_PASS:
+                sum_biases()
             if ready is not None:
-                multiply(stage - 1, *ready)
+                multiply(number - 1, *ready)
             ready = (x_codes, x_scales, w_codes, w_scales)
+            halves = next_halves
         quantise(*waiting)
-        multiply(STAGES - 1, *ready)
+        multiply(PASSES - 1, *ready)
 
         for c in range(MEMBERS):
-            add_chunk(total, products[c], c)
+            for j in range(MEMBERS):
+                nc.vector.tensor_tensor(
+                    out=total[:, j, :],
+                    in0=total[:, j, :],
+                    in1=products[c][:, j ^ c, :],
+                    op=ADD if SIGN[j][c] > 0 else SUBTRACT,
+                )
         nc.sync.dma_start(out=out, in_=total[:].rearrange("p j o -> p (j o)"))

@@ -27,6 +27,7 @@ BANK_MEMBERS = BANK_WORDS // (HALVES * P)
 LOAD_PASSES = (1, 1) + ((PASSES - 2) // 2) * (2,)
 RAW_BUFS = 6
 VECTOR_EVERY = 8
+MX_LAG = 2
 BIAS_PASS = 4
 
 SIGN = (
@@ -53,7 +54,7 @@ def tile_qdense_k_kernel(
         raw_pool = ctx.enter_context(tc.tile_pool(name="raw", bufs=RAW_BUFS))
         sorted_pool = ctx.enter_context(tc.tile_pool(name="sorted", bufs=4))
         grouped_pool = ctx.enter_context(tc.tile_pool(name="grouped", bufs=4))
-        code_pool = ctx.enter_context(tc.tile_pool(name="codes", bufs=3))
+        code_pool = ctx.enter_context(tc.tile_pool(name="codes", bufs=4))
         product_pool = ctx.enter_context(tc.psum_pool(name="products", bufs=1))
         bank_pool = ctx.enter_context(tc.psum_pool(name="banks", bufs=4))
 
@@ -156,7 +157,7 @@ def tile_qdense_k_kernel(
                 )
 
         waiting = None
-        ready = None
+        ready = []
         loads = 2
         halves = [sort_words(raw) for raw in raw_passes[0]]
         for number in range(PASSES):
@@ -178,12 +179,14 @@ def tile_qdense_k_kernel(
                     next_halves.append(sort_words(raw_passes[number + 1][operand]))
             if number == BIAS_PASS:
                 sum_biases()
-            if ready is not None:
-                multiply(number - 1, *ready)
-            ready = (x_codes, x_scales, w_codes, w_scales)
+            if len(ready) == MX_LAG:
+                multiply(*ready[0])
+                ready = ready[1:]
+            ready = ready + [(number, x_codes, x_scales, w_codes, w_scales)]
             halves = next_halves
         quantise(*waiting)
-        multiply(PASSES - 1, *ready)
+        for last in ready:
+            multiply(*last)
 
         for c in range(MEMBERS):
             for j in range(MEMBERS):

@@ -26,7 +26,6 @@ BANK_MEMBERS = BANK_WORDS // (HALVES * P)
 
 LOAD_PASSES = (1, 1) + ((PASSES - 2) // 2) * (2,)
 RAW_BUFS = 6
-VECTOR_EVERY = 8
 MX_LAG = 2
 BIAS_PASS = 4
 
@@ -118,7 +117,7 @@ def tile_qdense_k_kernel(
             )
             return halves
 
-        def transpose_pass(halves, first_bank):
+        def transpose_pass(halves):
             grouped = grouped_pool.tile([P, MEMBERS * P * PACK], BF16, align_bytes=64)
             grouped_words = grouped[:].bitcast(F32)
             for b in range(MEMBERS // BANK_MEMBERS):
@@ -130,9 +129,7 @@ def tile_qdense_k_kernel(
                             halves[:, u, b * BANK_MEMBERS + i, :].bitcast(F32),
                             identity[:],
                         )
-                to_vector = (first_bank + b) % VECTOR_EVERY == VECTOR_EVERY - 2
-                copy_out = nc.vector.tensor_copy if to_vector else nc.scalar.copy
-                copy_out(
+                nc.scalar.copy(
                     out=grouped_words[:, b * BANK_WORDS : (b + 1) * BANK_WORDS].rearrange(
                         "p (i r u) -> p i r u", i=BANK_MEMBERS, u=HALVES
                     ),
@@ -170,8 +167,7 @@ def tile_qdense_k_kernel(
             w_scales = code_pool.tile([P, MEMBERS * P], U8, align_bytes=64)
             next_halves = []
             for operand, (codes, scales) in enumerate(((x_codes, x_scales), (w_codes, w_scales))):
-                first_bank = (2 * number + operand) * (MEMBERS // BANK_MEMBERS)
-                grouped = transpose_pass(halves[operand], first_bank)
+                grouped = transpose_pass(halves[operand])
                 if waiting is not None:
                     quantise(*waiting)
                 waiting = (grouped, codes, scales)

@@ -27,6 +27,7 @@ BANK_MEMBERS = BANK_WORDS // (HALVES * P)
 LOAD_PASSES = (1, 1) + ((PASSES - 2) // 2) * (2,)
 RAW_BUFS = 6
 MX_LAG = 2
+SORT_AHEAD = 2
 BIAS_PASS = 4
 
 SIGN = (
@@ -51,7 +52,7 @@ def tile_qdense_k_kernel(
         ctx.enter_context(tc.manual_schedule())
         const = ctx.enter_context(tc.tile_pool(name="const", bufs=1))
         raw_pool = ctx.enter_context(tc.tile_pool(name="raw", bufs=RAW_BUFS))
-        sorted_pool = ctx.enter_context(tc.tile_pool(name="sorted", bufs=4))
+        sorted_pool = ctx.enter_context(tc.tile_pool(name="sorted", bufs=2 * (SORT_AHEAD + 1)))
         grouped_pool = ctx.enter_context(tc.tile_pool(name="grouped", bufs=4))
         code_pool = ctx.enter_context(tc.tile_pool(name="codes", bufs=4))
         product_pool = ctx.enter_context(tc.psum_pool(name="products", bufs=1))
@@ -156,30 +157,30 @@ def tile_qdense_k_kernel(
         waiting = None
         ready = []
         loads = 2
-        halves = [sort_words(raw) for raw in raw_passes[0]]
+        halves = [[sort_words(raw) for raw in raw_passes[g]] for g in range(SORT_AHEAD)]
         for number in range(PASSES):
-            if loads < len(LOAD_PASSES) and len(raw_passes) < number + 2 + LOAD_PASSES[loads]:
+            if loads < len(LOAD_PASSES) and len(raw_passes) < number + SORT_AHEAD + max(LOAD_PASSES):
                 raw_passes.extend(load(len(raw_passes), LOAD_PASSES[loads]))
                 loads += 1
             x_codes = code_pool.tile([P, MEMBERS * P], U32, align_bytes=64)
             x_scales = code_pool.tile([P, MEMBERS * P], U8, align_bytes=64)
             w_codes = code_pool.tile([P, MEMBERS * P], U32, align_bytes=64)
             w_scales = code_pool.tile([P, MEMBERS * P], U8, align_bytes=64)
-            next_halves = []
+            coming = number + SORT_AHEAD
+            halves.append([])
             for operand, (codes, scales) in enumerate(((x_codes, x_scales), (w_codes, w_scales))):
-                grouped = transpose_pass(halves[operand])
+                grouped = transpose_pass(halves[number][operand])
                 if waiting is not None:
                     quantise(*waiting)
                 waiting = (grouped, codes, scales)
-                if number + 1 < PASSES:
-                    next_halves.append(sort_words(raw_passes[number + 1][operand]))
+                if coming < PASSES:
+                    halves[coming].append(sort_words(raw_passes[coming][operand]))
             if number == BIAS_PASS:
                 sum_biases()
             if len(ready) == MX_LAG:
                 multiply(*ready[0])
                 ready = ready[1:]
             ready = ready + [(number, x_codes, x_scales, w_codes, w_scales)]
-            halves = next_halves
         quantise(*waiting)
         for last in ready:
             multiply(*last)

@@ -24,11 +24,13 @@ RUN = 16
 BANK_WORDS = 512
 BANK_MEMBERS = BANK_WORDS // (HALVES * P)
 
-LOAD_PASSES = (1, 1) + ((PASSES - 2) // 2) * (2,)
-RAW_BUFS = 6
+LOAD_PASSES = 10 * (3,) + (2,)
+RAW_BUFS = 4
+RUN_TILES = 2
+SORT_AHEAD = 2 * RUN_TILES
 MX_LAG = 2
-SORT_AHEAD = 2
-BIAS_PASS = 4
+BIAS_RUN = 4
+X, W = 0, 1
 
 SIGN = (
     (1, -1, -1, -1),
@@ -48,32 +50,38 @@ def tile_qdense_k_kernel(
     weights = (W_rr, W_ri, W_rj, W_rk)
     biases = (b_rr, b_ri, b_rj, b_rk)
 
+    firsts = [sum(LOAD_PASSES[:n]) for n in range(len(LOAD_PASSES))]
+    tiles = [
+        (n, operand, g, firsts[n] + g)
+        for n in range(len(LOAD_PASSES))
+        for operand in (X, W)
+        for g in range(LOAD_PASSES[n])
+    ]
+
     with ExitStack() as ctx:
         ctx.enter_context(tc.manual_schedule())
         const = ctx.enter_context(tc.tile_pool(name="const", bufs=1))
         raw_pool = ctx.enter_context(tc.tile_pool(name="raw", bufs=RAW_BUFS))
-        sorted_pool = ctx.enter_context(tc.tile_pool(name="sorted", bufs=2 * (SORT_AHEAD + 1)))
+        sorted_pool = ctx.enter_context(tc.tile_pool(name="sorted", bufs=SORT_AHEAD + RUN_TILES))
         grouped_pool = ctx.enter_context(tc.tile_pool(name="grouped", bufs=4))
-        code_pool = ctx.enter_context(tc.tile_pool(name="codes", bufs=4))
+        code_pools = (
+            ctx.enter_context(tc.tile_pool(name="x_codes", bufs=7)),
+            ctx.enter_context(tc.tile_pool(name="w_codes", bufs=6)),
+        )
         product_pool = ctx.enter_context(tc.psum_pool(name="products", bufs=1))
         bank_pool = ctx.enter_context(tc.psum_pool(name="banks", bufs=4))
 
-        def load(first_pass, passes):
-            width = passes * K_PASS
-            cols = slice(first_pass * K_PASS, first_pass * K_PASS + width)
+        def load(n):
+            width = LOAD_PASSES[n] * K_PASS
+            cols = slice(firsts[n] * K_PASS, firsts[n] * K_PASS + width)
             x_raw = raw_pool.tile([P, MEMBERS, max(LOAD_PASSES) * K_PASS], BF16, name="x_raw")
             nc.sync.dma_start(out=x_raw[:, :, :width], in_=x_chunks[:, :, cols])
             w_raw = raw_pool.tile([P, MEMBERS, max(LOAD_PASSES) * K_PASS], BF16, name="w_raw")
             for q in range(MEMBERS):
                 nc.sync.dma_start(out=w_raw[:, q, :width], in_=weights[q][:, cols])
-            return [
-                (x_raw[:, :, g * K_PASS : (g + 1) * K_PASS], w_raw[:, :, g * K_PASS : (g + 1) * K_PASS])
-                for g in range(passes)
-            ]
+            return x_raw, w_raw
 
-        raw_passes = []
-        for passes in LOAD_PASSES[:2]:
-            raw_passes.extend(load(len(raw_passes), passes))
+        loads = [load(0)]
 
         identity = const.tile([P, P], F32)
         masks.make_identity(nc, identity[:])
@@ -110,7 +118,10 @@ def tile_qdense_k_kernel(
             for c in range(MEMBERS)
         ]
 
-        def sort_words(raw):
+        def sort_words(n, operand, g):
+            for number in range(len(loads), min(n + RAW_BUFS, len(LOAD_PASSES))):
+                loads.append(load(number))
+            raw = loads[n][operand][:, :, g * K_PASS : (g + 1) * K_PASS]
             halves = sorted_pool.tile([P, HALVES, MEMBERS, K_HALF], BF16, name="halves")
             nc.vector.tensor_copy(
                 out=halves[:].rearrange("p u m (n e) -> p m n u e", e=RUN),
@@ -118,7 +129,7 @@ def tile_qdense_k_kernel(
             )
             return halves
 
-        def transpose_pass(halves):
+        def transpose_tile(halves):
             grouped = grouped_pool.tile([P, MEMBERS * P * PACK], BF16, align_bytes=64)
             grouped_words = grouped[:].bitcast(F32)
             for b in range(MEMBERS // BANK_MEMBERS):
@@ -141,7 +152,9 @@ def tile_qdense_k_kernel(
         def quantise(grouped, codes, scales):
             nc.vector.quantize_mx(out=codes[:].bitcast(FP8X4), scales=scales[:], in_=grouped[:])
 
-        def multiply(number, x_codes, x_scales, w_codes, w_scales):
+        def multiply(number):
+            x_codes, x_scales = quantised[number, X]
+            w_codes, w_scales = quantised[number, W]
             for c in range(MEMBERS):
                 rows = slice(c * P, (c + 1) * P)
                 nc.tensor.matmul_mx(
@@ -154,36 +167,33 @@ def tile_qdense_k_kernel(
                     stop=(number == PASSES - 1),
                 )
 
+        halves = [sort_words(*tile[:3]) for tile in tiles[:SORT_AHEAD]]
         waiting = None
-        ready = []
-        loads = 2
-        halves = [[sort_words(raw) for raw in raw_passes[g]] for g in range(SORT_AHEAD)]
-        for number in range(PASSES):
-            if loads < len(LOAD_PASSES) and len(raw_passes) < number + SORT_AHEAD + max(LOAD_PASSES):
-                raw_passes.extend(load(len(raw_passes), LOAD_PASSES[loads]))
-                loads += 1
-            x_codes = code_pool.tile([P, MEMBERS * P], U32, align_bytes=64)
-            x_scales = code_pool.tile([P, MEMBERS * P], U8, align_bytes=64)
-            w_codes = code_pool.tile([P, MEMBERS * P], U32, align_bytes=64)
-            w_scales = code_pool.tile([P, MEMBERS * P], U8, align_bytes=64)
-            coming = number + SORT_AHEAD
-            halves.append([])
-            for operand, (codes, scales) in enumerate(((x_codes, x_scales), (w_codes, w_scales))):
-                grouped = transpose_pass(halves[number][operand])
-                if waiting is not None:
-                    quantise(*waiting)
-                waiting = (grouped, codes, scales)
-                if coming < PASSES:
-                    halves[coming].append(sort_words(raw_passes[coming][operand]))
-            if number == BIAS_PASS:
-                sum_biases()
-            if len(ready) == MX_LAG:
-                multiply(*ready[0])
-                ready = ready[1:]
-            ready = ready + [(number, x_codes, x_scales, w_codes, w_scales)]
+        quantised = {}
+        last_runs = {}
+        multiplied = 0
+        for t, (n, operand, g, number) in enumerate(tiles):
+            run = t // RUN_TILES
+            grouped = transpose_tile(halves[t])
+            if waiting is not None:
+                quantise(*waiting)
+            codes = code_pools[operand].tile([P, MEMBERS * P], U32, align_bytes=64, name="codes")
+            scales = code_pools[operand].tile([P, MEMBERS * P], U8, align_bytes=64, name="scales")
+            quantised[number, operand] = (codes, scales)
+            waiting = (grouped, codes, scales)
+            if operand == W:
+                last_runs[number] = run
+            if t + SORT_AHEAD < len(tiles):
+                halves.append(sort_words(*tiles[t + SORT_AHEAD][:3]))
+            if t % RUN_TILES == RUN_TILES - 1:
+                if run == BIAS_RUN:
+                    sum_biases()
+                if last_runs.get(multiplied, run) <= run - MX_LAG:
+                    multiply(multiplied)
+                    multiplied += 1
         quantise(*waiting)
-        for last in ready:
-            multiply(*last)
+        for number in range(multiplied, PASSES):
+            multiply(number)
 
         for c in range(MEMBERS):
             for j in range(MEMBERS):

@@ -63,7 +63,7 @@ def tile_qdense_k_kernel(
         const = ctx.enter_context(tc.tile_pool(name="const", bufs=1))
         raw_pool = ctx.enter_context(tc.tile_pool(name="raw", bufs=RAW_BUFS))
         sorted_pool = ctx.enter_context(tc.tile_pool(name="sorted", bufs=SORT_AHEAD + RUN_TILES))
-        grouped_pool = ctx.enter_context(tc.tile_pool(name="grouped", bufs=4))
+        grouped_pool = ctx.enter_context(tc.tile_pool(name="grouped", bufs=6))
         code_pools = (
             ctx.enter_context(tc.tile_pool(name="x_codes", bufs=7)),
             ctx.enter_context(tc.tile_pool(name="w_codes", bufs=6)),

from contextlib import ExitStack

import concourse.masks as masks
import concourse.mybir as mybir

F32 = mybir.dt.float32
BF16 = mybir.dt.bfloat16
U32 = mybir.dt.uint32
U8 = mybir.dt.uint8
FP8X4 = mybir.dt.float8_e4m3fn_x4
ADD = mybir.AluOpType.add
SUBTRACT = mybir.AluOpType.subtract

P = 128
QUADRANT = 32
MEMBERS = 4
K = 16384
PACK = 4
K_PASS = P * PACK
PASSES = K // K_PASS
HALVES = 2
K_HALF = K_PASS // HALVES
RUN = 16
BANK_WORDS = 512
BANK_MEMBERS = BANK_WORDS // (HALVES * P)

LOAD_PASSES = 10 * (3,) + (2,)
RAW_BUFS = 4
RUN_TILES = 2
SORT_AHEAD = 2 * RUN_TILES
MX_LAG = 2
BIAS_RUN = 4
X, W = 0, 1

SIGN = (
    (1, -1, -1, -1),
    (1, 1, 1, -1),
    (1, -1, 1, 1),
    (1, 1, -1, 1),
)

FLOPS = 2 * (MEMBERS * P) * (MEMBERS * P) * K


def tile_qdense_k_kernel(
    tc, x, W_rr, W_ri, W_rj, W_rk, b_rr, b_ri, b_rj, b_rk, out
):
    nc = tc.nc
    x_chunks = x.rearrange("b (c k) -> b c k", c=MEMBERS)
    weights = (W_rr, W_ri, W_rj, W_rk)
    biases = (b_rr, b_ri, b_rj, b_rk)

    firsts = [sum(LOAD_PASSES[:n]) for n in range(len(LOAD_PASSES))]
    tiles = [
        (n, operand, g, firsts[n] + g)
        for n in range(len(LOAD_PASSES))
        for operand in (X, W)
        for g in range(LOAD_PASSES[n])
    ]

    with ExitStack() as ctx:
        ctx.enter_context(tc.manual_schedule())
        const = ctx.enter_context(tc.tile_pool(name="const", bufs=1))
        raw_pool = ctx.enter_context(tc.tile_pool(name="raw", bufs=RAW_BUFS))
        sorted_pool = ctx.enter_context(tc.tile_pool(name="sorted", bufs=SORT_AHEAD + RUN_TILES))
        grouped_pool = ctx.enter_context(tc.tile_pool(name="grouped", bufs=6))
        code_pools = (
            ctx.enter_context(tc.tile_pool(name="x_codes", bufs=7)),
            ctx.enter_context(tc.tile_pool(name="w_codes", bufs=6)),
        )
        product_pool = ctx.enter_context(tc.psum_pool(name="products", bufs=1))
        bank_pool = ctx.enter_context(tc.psum_pool(name="banks", bufs=4))

        def load(n):
            width = LOAD_PASSES[n] * K_PASS
            cols = slice(firsts[n] * K_PASS, firsts[n] * K_PASS + width)
            x_raw = raw_pool.tile([P, MEMBERS, max(LOAD_PASSES) * K_PASS], BF16, name="x_raw")
            nc.sync.dma_start(out=x_raw[:, :, :width], in_=x_chunks[:, :, cols])
            w_raw = raw_pool.tile([P, MEMBERS, max(LOAD_PASSES) * K_PASS], BF16, name="w_raw")
            for q in range(MEMBERS):
                nc.sync.dma_start(out=w_raw[:, q, :width], in_=weights[q][:, cols])
            return x_raw, w_raw

        loads = [load(0)]

        identity = const.tile([P, P], F32)
        masks.make_identity(nc, identity[:])

        bias_rows = const.tile([P, P], BF16)
        nc.gpsimd.memset(bias_rows[:], 0.0)
        for q in range(MEMBERS):
            nc.sync.dma_start(
                out=bias_rows[QUADRANT * q : QUADRANT * q + 1, :], in_=biases[q].unsqueeze(0)
            )
        bias_signs = const.tile([P, MEMBERS], BF16)
        for q in range(MEMBERS):
            for j in range(MEMBERS):
                nc.gpsimd.memset(
                    bias_signs[QUADRANT * q : QUADRANT * (q + 1), j : j + 1],
                    float(SIGN[j][j ^ q]),
                )
        total = const.tile([P, MEMBERS, P], F32)

        def sum_biases():
            bank = bank_pool.tile([P, MEMBERS, P], F32, tag="bank")
            for j in range(MEMBERS):
                nc.tensor.matmul(
                    out=bank[:, j, :],
                    lhsT=bias_signs[:, j : j + 1].to_broadcast([P, P]),
                    rhs=bias_rows[:],
                    start=True,
                    stop=True,
                )
            nc.scalar.copy(out=total[:], in_=bank[:])

        products = [
            product_pool.tile([P, MEMBERS, P], F32, name="products%d" % c)
            for c in range(MEMBERS)
        ]

        def sort_words(n, operand, g):
            for number in range(len(loads), min(n + RAW_BUFS, len(LOAD_PASSES))):
                loads.append(load(number))
            raw = loads[n][operand][:, :, g * K_PASS : (g + 1) * K_PASS]
            halves = sorted_pool.tile([P, HALVES, MEMBERS, K_HALF], BF16, name="halves")
            nc.vector.tensor_copy(
                out=halves[:].rearrange("p u m (n e) -> p m n u e", e=RUN),
                in_=raw.rearrange("p m (n u e) -> p m n u e", u=HALVES, e=RUN),
            )
            return halves

        def transpose_tile(halves):
            grouped = grouped_pool.tile([P, MEMBERS * P * PACK], BF16, align_bytes=64)
            grouped_words = grouped[:].bitcast(F32)
            for b in range(MEMBERS // BANK_MEMBERS):
                bank = bank_pool.tile([P, BANK_MEMBERS, HALVES, P], F32, tag="bank")
                for i in range(BANK_MEMBERS):
                    for u in range(HALVES):
                        nc.tensor.transpose(
                            bank[:, i, u, :],
                            halves[:, u, b * BANK_MEMBERS + i, :].bitcast(F32),
                            identity[:],
                        )
                nc.scalar.copy(
                    out=grouped_words[:, b * BANK_WORDS : (b + 1) * BANK_WORDS].rearrange(
                        "p (i r u) -> p i r u", i=BANK_MEMBERS, u=HALVES
                    ),
                    in_=bank[:].rearrange("p i u r -> p i r u"),
                )
            return grouped

        def quantise(grouped, codes, scales):
            nc.vector.quantize_mx(out=codes[:].bitcast(FP8X4), scales=scales[:], in_=grouped[:])

        def multiply(number):
            x_codes, x_scales = quantised[number, X]
            w_codes, w_scales = quantised[number, W]
            for c in range(MEMBERS):
                rows = slice(c * P, (c + 1) * P)
                nc.tensor.matmul_mx(
                    out=products[c][:].rearrange("p q o -> p (q o)"),
                    lhsT=x_codes[:, rows].bitcast(FP8X4),
                    lhsT_scale=x_scales[:, rows],
                    rhs=w_codes[:].bitcast(FP8X4),
                    rhs_scale=w_scales[:],
                    start=(number == 0),
                    stop=(number == PASSES - 1),
                )

        halves = [sort_words(*tile[:3]) for tile in tiles[:SORT_AHEAD]]
        waiting = None
        quantised = {}
        last_runs = {}
        multiplied = 0
        for t, (n, operand, g, number) in enumerate(tiles):
            run = t // RUN_TILES
            grouped = transpose_tile(halves[t])
            if waiting is not None:
                quantise(*waiting)
            codes = code_pools[operand].tile([P, MEMBERS * P], U32, align_bytes=64, name="codes")
            scales = code_pools[operand].tile([P, MEMBERS * P], U8, align_bytes=64, name="scales")
            quantised[number, operand] = (codes, scales)
            waiting = (grouped, codes, scales)
            if operand == W:
                last_runs[number] = run
            if t + SORT_AHEAD < len(tiles):
                halves.append(sort_words(*tiles[t + SORT_AHEAD][:3]))
            if t % RUN_TILES == RUN_TILES - 1:
                if run == BIAS_RUN:
                    sum_biases()
                if last_runs.get(multiplied, run) <= run - MX_LAG:
                    multiply(multiplied)
                    multiplied += 1
        quantise(*waiting)
        for number in range(multiplied, PASSES):
            multiply(number)

        for c in range(MEMBERS):
            for j in range(MEMBERS):
                nc.vector.tensor_tensor(
                    out=total[:, j, :],
                    in0=total[:, j, :],
                    in1=products[c][:, j ^ c, :],
                    op=ADD if SIGN[j][c] > 0 else SUBTRACT,
                )
        nc.sync.dma_start(out=out, in_=total[:].rearrange("p j o -> p (j o)"))
